import numpy as np
import ml_dtypes

BF16 = ml_dtypes.bfloat16


def bf(x):
    return np.asarray(x, np.float32).astype(BF16)


def f32(x):
    return np.asarray(x, np.float32)


def f64(x):
    return np.asarray(x).astype(np.float64)


def striped(idx):
    return np.tile(idx.reshape(-1, 16).T, (8, 1))


C, S, N = 128, 4096, 1024


def sigmoid(v):
    return 1.0 / (1.0 + np.exp(-v))


def setup_inputs():
    return {"z": f32(np.random.standard_normal((C, N))), "zr": f32(np.random.standard_normal((C, S))), "rb": f32(0.1 * np.random.standard_normal((C, 1))), "offs": striped(np.random.permutation(S)[:N])}


def reference(z, zr, rb, offs):
    idx = offs[:16].T.reshape(-1)
    u = 1.0 / sigmoid(f64(zr) + f64(rb))
    return np.log(u[:, idx] * sigmoid(f64(z)))

@@ -1,0 +1,65 @@
+import concourse.mybir as mybir
+
+F32 = mybir.dt.float32
+U16 = mybir.dt.uint16
+FUNC = mybir.ActivationFunctionType
+MULT = mybir.AluOpType.mult
+
+LABELS = 128
+STORE = 4096
+BATCH = 1024
+
+CHUNK = 512
+PIECE = 256
+PER_COLUMN = 16
+
+
+def tile_visionmodelforcls_kernel(tc, z, zr, rb, offs, out):
+    nc = tc.nc
+    queues = (nc.sync, nc.scalar)
+
+    with tc.tile_pool(name="held", bufs=1) as held:
+        z_sb = held.tile([LABELS, BATCH], F32, name="z_sb")
+        half = BATCH // 2
+        for h in range(2):
+            cols = slice(h * half, (h + 1) * half)
+            queues[h].dma_start(z_sb[:, cols], z[:, cols])
+
+        rb_sb = held.tile([LABELS, 1], F32, name="rb_sb")
+        nc.sync.dma_start(rb_sb[:], rb)
+
+        zr_sb = held.tile([LABELS, STORE], F32, name="zr_sb")
+        for k in range(STORE // CHUNK):
+            cols = slice(k * CHUNK, (k + 1) * CHUNK)
+            queues[k % 2].dma_start(zr_sb[:, cols], zr[:, cols])
+
+        offsets = held.tile([LABELS, BATCH // PER_COLUMN], U16, name="offsets")
+        nc.sync.dma_start(offsets[:], offs)
+
+        score = held.tile([LABELS, BATCH], F32, name="score")
+        for h in range(2):
+            cols = slice(h * half, (h + 1) * half)
+            nc.scalar.activation(score[:, cols], z_sb[:, cols], FUNC.Sigmoid)
+
+        minus_rb = held.tile([LABELS, 1], F32, name="minus_rb")
+        nc.vector.tensor_scalar_mul(minus_rb[:], rb_sb[:], -1.0)
+
+        decay = held.tile([LABELS, STORE], F32, name="decay")
+        u = held.tile([LABELS, STORE], F32, name="u")
+        for k in range(STORE // CHUNK):
+            cols = slice(k * CHUNK, (k + 1) * CHUNK)
+            nc.scalar.activation(
+                decay[:, cols], zr_sb[:, cols], FUNC.Exp, bias=minus_rb[:], scale=-1.0
+            )
+            nc.vector.tensor_scalar_add(u[:, cols], decay[:, cols], 1.0)
+
+        ratio = held.tile([LABELS, BATCH], F32, name="ratio")
+        log_ratio = held.tile([LABELS, BATCH], F32, name="log_ratio")
+        for p in range(BATCH // PIECE):
+            cols = slice(p * PIECE, (p + 1) * PIECE)
+            entries = slice(p * PIECE // PER_COLUMN, (p + 1) * PIECE // PER_COLUMN)
+            nc.vector.tensor_tensor(
+                ratio[:, cols], u[:].indirect(offsets[:, entries]), score[:, cols], MULT
+            )
+            nc.scalar.activation(log_ratio[:, cols], ratio[:, cols], FUNC.Ln)
+            nc.sync.dma_start(out[:, cols], log_ratio[:, cols])

@@ -19,6 +19,11 @@ def tile_visionmodelforcls_kernel(tc, z, zr, rb, offs, out):
     queues = (nc.sync, nc.scalar)
 
     with tc.tile_pool(name="held", bufs=1) as held:
+        idle_in = held.tile([LABELS, 1], F32, name="idle_in")
+        idle_out = held.tile([LABELS, 1], F32, name="idle_out")
+        nc.vector.memset(idle_in[:], 0.0)
+        nc.scalar.activation(idle_out[:], idle_in[:], FUNC.Sigmoid)
+
         z_sb = held.tile([LABELS, BATCH], F32, name="z_sb")
         half = BATCH // 2
         for h in range(2):

@@ -16,19 +16,12 @@ PER_COLUMN = 16
 
 def tile_visionmodelforcls_kernel(tc, z, zr, rb, offs, out):
     nc = tc.nc
-    queues = (nc.sync, nc.scalar)
 
     with tc.tile_pool(name="held", bufs=1) as held:
         idle_in = held.tile([LABELS, 1], F32, name="idle_in")
         idle_out = held.tile([LABELS, 1], F32, name="idle_out")
         nc.vector.memset(idle_in[:], 0.0)
-        nc.scalar.activation(idle_out[:], idle_in[:], FUNC.Sigmoid)
-
-        z_sb = held.tile([LABELS, BATCH], F32, name="z_sb")
-        half = BATCH // 2
-        for h in range(2):
-            cols = slice(h * half, (h + 1) * half)
-            queues[h].dma_start(z_sb[:, cols], z[:, cols])
+        nc.scalar.activation(idle_out[:], idle_in[:], FUNC.Exp)
 
         rb_sb = held.tile([LABELS, 1], F32, name="rb_sb")
         nc.sync.dma_start(rb_sb[:], rb)
@@ -36,15 +29,13 @@ def tile_visionmodelforcls_kernel(tc, z, zr, rb, offs, out):
         zr_sb = held.tile([LABELS, STORE], F32, name="zr_sb")
         for k in range(STORE // CHUNK):
             cols = slice(k * CHUNK, (k + 1) * CHUNK)
-            queues[k % 2].dma_start(zr_sb[:, cols], zr[:, cols])
+            nc.sync.dma_start(zr_sb[:, cols], zr[:, cols])
+
+        z_sb = held.tile([LABELS, BATCH], F32, name="z_sb")
+        nc.sync.dma_start(z_sb[:], z)
 
         offsets = held.tile([LABELS, BATCH // PER_COLUMN], U16, name="offsets")
         nc.sync.dma_start(offsets[:], offs)
-
-        score = held.tile([LABELS, BATCH], F32, name="score")
-        for h in range(2):
-            cols = slice(h * half, (h + 1) * half)
-            nc.scalar.activation(score[:, cols], z_sb[:, cols], FUNC.Sigmoid)
 
         minus_rb = held.tile([LABELS, 1], F32, name="minus_rb")
         nc.vector.tensor_scalar_mul(minus_rb[:], rb_sb[:], -1.0)
@@ -57,6 +48,11 @@ def tile_visionmodelforcls_kernel(tc, z, zr, rb, offs, out):
                 decay[:, cols], zr_sb[:, cols], FUNC.Exp, bias=minus_rb[:], scale=-1.0
             )
             nc.vector.tensor_scalar_add(u[:, cols], decay[:, cols], 1.0)
+
+        score = held.tile([LABELS, BATCH], F32, name="score")
+        for p in range(BATCH // PIECE):
+            cols = slice(p * PIECE, (p + 1) * PIECE)
+            nc.scalar.activation(score[:, cols], z_sb[:, cols], FUNC.Sigmoid)
 
         ratio = held.tile([LABELS, BATCH], F32, name="ratio")
         log_ratio = held.tile([LABELS, BATCH], F32, name="log_ratio")

@@ -3,15 +3,25 @@ import concourse.mybir as mybir
 F32 = mybir.dt.float32
 U16 = mybir.dt.uint16
 FUNC = mybir.ActivationFunctionType
-MULT = mybir.AluOpType.mult
+ALU = mybir.AluOpType
 
 LABELS = 128
 STORE = 4096
 BATCH = 1024
 
 CHUNK = 512
+CHUNKS = (512,) * 7 + (256, 128, 128)
 PIECE = 256
 PER_COLUMN = 16
+
+
+def spans(widths):
+    slices = []
+    first = 0
+    for width in widths:
+        slices.append(slice(first, first + width))
+        first += width
+    return slices
 
 
 def tile_visionmodelforcls_kernel(tc, z, zr, rb, offs, out):
@@ -26,33 +36,45 @@ def tile_visionmodelforcls_kernel(tc, z, zr, rb, offs, out):
         rb_sb = held.tile([LABELS, 1], F32, name="rb_sb")
         nc.sync.dma_start(rb_sb[:], rb)
 
-        zr_sb = held.tile([LABELS, STORE], F32, name="zr_sb")
-        for k in range(STORE // CHUNK):
-            cols = slice(k * CHUNK, (k + 1) * CHUNK)
-            nc.sync.dma_start(zr_sb[:, cols], zr[:, cols])
-
         z_sb = held.tile([LABELS, BATCH], F32, name="z_sb")
-        nc.sync.dma_start(z_sb[:], z)
+        for k in range(BATCH // CHUNK):
+            cols = slice(k * CHUNK, (k + 1) * CHUNK)
+            nc.sync.dma_start(z_sb[:, cols], z[:, cols])
 
         offsets = held.tile([LABELS, BATCH // PER_COLUMN], U16, name="offsets")
         nc.sync.dma_start(offsets[:], offs)
 
+        zr_sb = held.tile([LABELS, STORE], F32, name="zr_sb")
+        for cols in spans(CHUNKS):
+            nc.sync.dma_start(zr_sb[:, cols], zr[:, cols])
+
         minus_rb = held.tile([LABELS, 1], F32, name="minus_rb")
         nc.vector.tensor_scalar_mul(minus_rb[:], rb_sb[:], -1.0)
 
+        tanh_half = held.tile([LABELS, BATCH], F32, name="tanh_half")
+        exp_z = held.tile([LABELS, BATCH], F32, name="exp_z")
+        abs_tanh = held.tile([LABELS, BATCH], F32, name="abs_tanh")
+        upper = held.tile([LABELS, BATCH], F32, name="upper")
+        score = held.tile([LABELS, BATCH], F32, name="score")
+        for k in range(BATCH // CHUNK):
+            cols = slice(k * CHUNK, (k + 1) * CHUNK)
+            nc.scalar.activation(tanh_half[:, cols], z_sb[:, cols], FUNC.Tanh, scale=0.5)
+            nc.scalar.activation(exp_z[:, cols], z_sb[:, cols], FUNC.Exp)
+            nc.vector.scalar_tensor_tensor(
+                abs_tanh[:, cols], tanh_half[:, cols], -1.0, tanh_half[:, cols], ALU.mult, ALU.max
+            )
+            nc.vector.tensor_scalar(upper[:, cols], abs_tanh[:, cols], 0.5, 0.5, ALU.mult, ALU.add)
+            nc.vector.scalar_tensor_tensor(
+                score[:, cols], exp_z[:, cols], 1.0, upper[:, cols], ALU.min, ALU.mult
+            )
+
         decay = held.tile([LABELS, STORE], F32, name="decay")
         u = held.tile([LABELS, STORE], F32, name="u")
-        for k in range(STORE // CHUNK):
-            cols = slice(k * CHUNK, (k + 1) * CHUNK)
+        for cols in spans(CHUNKS):
             nc.scalar.activation(
                 decay[:, cols], zr_sb[:, cols], FUNC.Exp, bias=minus_rb[:], scale=-1.0
             )
             nc.vector.tensor_scalar_add(u[:, cols], decay[:, cols], 1.0)
-
-        score = held.tile([LABELS, BATCH], F32, name="score")
-        for p in range(BATCH // PIECE):
-            cols = slice(p * PIECE, (p + 1) * PIECE)
-            nc.scalar.activation(score[:, cols], z_sb[:, cols], FUNC.Sigmoid)
 
         ratio = held.tile([LABELS, BATCH], F32, name="ratio")
         log_ratio = held.tile([LABELS, BATCH], F32, name="log_ratio")
@@ -60,7 +82,7 @@ def tile_visionmodelforcls_kernel(tc, z, zr, rb, offs, out):
             cols = slice(p * PIECE, (p + 1) * PIECE)
             entries = slice(p * PIECE // PER_COLUMN, (p + 1) * PIECE // PER_COLUMN)
             nc.vector.tensor_tensor(
-                ratio[:, cols], u[:].indirect(offsets[:, entries]), score[:, cols], MULT
+                ratio[:, cols], u[:].indirect(offsets[:, entries]), score[:, cols], ALU.mult
             )
             nc.scalar.activation(log_ratio[:, cols], ratio[:, cols], FUNC.Ln)
             nc.sync.dma_start(out[:, cols], log_ratio[:, cols])

@@ -10,7 +10,7 @@ STORE = 4096
 BATCH = 1024
 
 CHUNK = 512
-CHUNKS = (512,) * 7 + (256, 128, 128)
+CHUNKS = (1024, 1024, 1024, 512, 256, 128, 128)
 PIECE = 256
 PER_COLUMN = 16
 

@@ -33,13 +33,13 @@ def tile_visionmodelforcls_kernel(tc, z, zr, rb, offs, out):
         nc.vector.memset(idle_in[:], 0.0)
         nc.scalar.activation(idle_out[:], idle_in[:], FUNC.Exp)
 
-        rb_sb = held.tile([LABELS, 1], F32, name="rb_sb")
-        nc.sync.dma_start(rb_sb[:], rb)
-
         z_sb = held.tile([LABELS, BATCH], F32, name="z_sb")
         for k in range(BATCH // CHUNK):
             cols = slice(k * CHUNK, (k + 1) * CHUNK)
             nc.sync.dma_start(z_sb[:, cols], z[:, cols])
+
+        rb_sb = held.tile([LABELS, 1], F32, name="rb_sb")
+        nc.sync.dma_start(rb_sb[:], rb)
 
         offsets = held.tile([LABELS, BATCH // PER_COLUMN], U16, name="offsets")
         nc.sync.dma_start(offsets[:], offs)

@@ -28,11 +28,6 @@ def tile_visionmodelforcls_kernel(tc, z, zr, rb, offs, out):
     nc = tc.nc
 
     with tc.tile_pool(name="held", bufs=1) as held:
-        idle_in = held.tile([LABELS, 1], F32, name="idle_in")
-        idle_out = held.tile([LABELS, 1], F32, name="idle_out")
-        nc.vector.memset(idle_in[:], 0.0)
-        nc.scalar.activation(idle_out[:], idle_in[:], FUNC.Exp)
-
         z_sb = held.tile([LABELS, BATCH], F32, name="z_sb")
         for k in range(BATCH // CHUNK):
             cols = slice(k * CHUNK, (k + 1) * CHUNK)

@@ -11,7 +11,7 @@ BATCH = 1024
 
 CHUNK = 512
 CHUNKS = (1024, 1024, 1024, 512, 256, 128, 128)
-PIECE = 256
+PIECES = (384, 384, 128, 128)
 PER_COLUMN = 16
 
 
@@ -73,9 +73,8 @@ def tile_visionmodelforcls_kernel(tc, z, zr, rb, offs, out):
 
         ratio = held.tile([LABELS, BATCH], F32, name="ratio")
         log_ratio = held.tile([LABELS, BATCH], F32, name="log_ratio")
-        for p in range(BATCH // PIECE):
-            cols = slice(p * PIECE, (p + 1) * PIECE)
-            entries = slice(p * PIECE // PER_COLUMN, (p + 1) * PIECE // PER_COLUMN)
+        for cols in spans(PIECES):
+            entries = slice(cols.start // PER_COLUMN, cols.stop // PER_COLUMN)
             nc.vector.tensor_tensor(
                 ratio[:, cols], u[:].indirect(offsets[:, entries]), score[:, cols], ALU.mult
             )

@@ -10,7 +10,7 @@ STORE = 4096
 BATCH = 1024
 
 CHUNK = 512
-CHUNKS = (1024, 1024, 1024, 512, 256, 128, 128)
+CHUNKS = (1024, 896, 768, 640, 384, 256, 128)
 PIECES = (384, 384, 128, 128)
 PER_COLUMN = 16
 

import concourse.mybir as mybir

F32 = mybir.dt.float32
U16 = mybir.dt.uint16
FUNC = mybir.ActivationFunctionType
ALU = mybir.AluOpType

LABELS = 128
STORE = 4096
BATCH = 1024

CHUNK = 512
CHUNKS = (1024, 896, 768, 640, 384, 256, 128)
PIECES = (384, 384, 128, 128)
PER_COLUMN = 16


def spans(widths):
    slices = []
    first = 0
    for width in widths:
        slices.append(slice(first, first + width))
        first += width
    return slices


def tile_visionmodelforcls_kernel(tc, z, zr, rb, offs, out):
    nc = tc.nc

    with tc.tile_pool(name="held", bufs=1) as held:
        z_sb = held.tile([LABELS, BATCH], F32, name="z_sb")
        for k in range(BATCH // CHUNK):
            cols = slice(k * CHUNK, (k + 1) * CHUNK)
            nc.sync.dma_start(z_sb[:, cols], z[:, cols])

        rb_sb = held.tile([LABELS, 1], F32, name="rb_sb")
        nc.sync.dma_start(rb_sb[:], rb)

        offsets = held.tile([LABELS, BATCH // PER_COLUMN], U16, name="offsets")
        nc.sync.dma_start(offsets[:], offs)

        zr_sb = held.tile([LABELS, STORE], F32, name="zr_sb")
        for cols in spans(CHUNKS):
            nc.sync.dma_start(zr_sb[:, cols], zr[:, cols])

        minus_rb = held.tile([LABELS, 1], F32, name="minus_rb")
        nc.vector.tensor_scalar_mul(minus_rb[:], rb_sb[:], -1.0)

        tanh_half = held.tile([LABELS, BATCH], F32, name="tanh_half")
        exp_z = held.tile([LABELS, BATCH], F32, name="exp_z")
        abs_tanh = held.tile([LABELS, BATCH], F32, name="abs_tanh")
        upper = held.tile([LABELS, BATCH], F32, name="upper")
        score = held.tile([LABELS, BATCH], F32, name="score")
        for k in range(BATCH // CHUNK):
            cols = slice(k * CHUNK, (k + 1) * CHUNK)
            nc.scalar.activation(tanh_half[:, cols], z_sb[:, cols], FUNC.Tanh, scale=0.5)
            nc.scalar.activation(exp_z[:, cols], z_sb[:, cols], FUNC.Exp)
            nc.vector.scalar_tensor_tensor(
                abs_tanh[:, cols], tanh_half[:, cols], -1.0, tanh_half[:, cols], ALU.mult, ALU.max
            )
            nc.vector.tensor_scalar(upper[:, cols], abs_tanh[:, cols], 0.5, 0.5, ALU.mult, ALU.add)
            nc.vector.scalar_tensor_tensor(
                score[:, cols], exp_z[:, cols], 1.0, upper[:, cols], ALU.min, ALU.mult
            )

        decay = held.tile([LABELS, STORE], F32, name="decay")
        u = held.tile([LABELS, STORE], F32, name="u")
        for cols in spans(CHUNKS):
            nc.scalar.activation(
                decay[:, cols], zr_sb[:, cols], FUNC.Exp, bias=minus_rb[:], scale=-1.0
            )
            nc.vector.tensor_scalar_add(u[:, cols], decay[:, cols], 1.0)

        ratio = held.tile([LABELS, BATCH], F32, name="ratio")
        log_ratio = held.tile([LABELS, BATCH], F32, name="log_ratio")
        for cols in spans(PIECES):
            entries = slice(cols.start // PER_COLUMN, cols.stop // PER_COLUMN)
            nc.vector.tensor_tensor(
                ratio[:, cols], u[:].indirect(offsets[:, entries]), score[:, cols], ALU.mult
            )
            nc.scalar.activation(log_ratio[:, cols], ratio[:, cols], FUNC.Ln)
            nc.sync.dma_start(out[:, cols], log_ratio[:, cols])
